import numpy as np
import ml_dtypes


def mxq(x, axis, fmt="e4m3"):
    dtype, down = {"e4m3": (ml_dtypes.float8_e4m3fn, 7), "e5m2": (ml_dtypes.float8_e5m2, 14)}[fmt]
    v = np.moveaxis(np.asarray(x, np.float32).astype(ml_dtypes.bfloat16).astype(np.float64), axis, -1)
    blocks = v.reshape(v.shape[:-1] + (-1, 32))
    amax = np.abs(blocks).max(-1, keepdims=True)
    byte = np.maximum(np.where(amax > 0, np.frexp(amax)[1] - 1 + 127, 0) - down, 1)
    scale = np.exp2(byte - 127.0)
    codes = (blocks / scale).astype(np.float32).astype(dtype).astype(np.float64)
    return np.moveaxis((codes * scale).reshape(v.shape), -1, axis)


WIDE = False


def mx_kscale(k):
    if not WIDE:
        return np.ones(k)
    levels = np.array([30, -30])
    if k % 512:
        return np.exp2(np.random.permutation(np.resize(levels, k // 32))).repeat(32)
    a = np.empty((k // 512, 16))
    for p in range(k // 512):
        a[p, :8] = np.random.permutation(np.resize(levels, 8))
        for g in range(8):
            far = levels[np.abs(levels - a[p, g]) >= 10]
            a[p, g + 8] = far[np.random.randint(len(far))]
    return np.exp2(a.ravel()).repeat(32)


BF16 = ml_dtypes.bfloat16


def bf(x):
    return np.asarray(x, np.float32).astype(BF16)


def f64(x):
    return np.asarray(x).astype(np.float64)


B, FG, HG, WG, K, DIM, NH, M = 1, 4, 16, 16, 1536, 1536, 12, 32
S = FG * HG * WG
D = DIM // NH
C = D // 2
C1 = C // 3
C0 = C - 2 * C1
EPS = 1e-06


def rmsnorm(v, g):
    return v / np.sqrt(np.mean(v * v, axis=-1, keepdims=True) + EPS) * g


def grid(t):
    tf, th, tw = t[:, :C0], t[:, C0:C0 + C1], t[:, C0 + C1:]
    g = np.concatenate([
        np.broadcast_to(tf[:FG, None, None, :], (FG, HG, WG, C0)),
        np.broadcast_to(th[None, :HG, None, :], (FG, HG, WG, C1)),
        np.broadcast_to(tw[None, None, :WG, :], (FG, HG, WG, C1)),
    ], axis=-1)
    return g.reshape(S, 1, C)


def rope(v, fc, fs):
    p = v.reshape(B, S, NH, C, 2)
    vr, vi = p[..., 0], p[..., 1]
    return np.stack([vr * fc - vi * fs, vr * fs + vi * fc], axis=-1).reshape(B, S, NH, D)


def setup_inputs():
    s = mx_kscale(K)
    theta = np.random.uniform(0.0, 2.0 * np.pi, (M, C))
    return {"x": bf(np.random.standard_normal((B, S, K)) * s),
            "wq": bf(np.random.standard_normal((DIM, K)) / np.sqrt(K) / s),
            "bq": bf(np.random.standard_normal(DIM) * 0.3),
            "wk": bf(np.random.standard_normal((DIM, K)) / np.sqrt(K) / s),
            "bk": bf(np.random.standard_normal(DIM) * 0.3),
            "gq": bf(1.0 + 0.1 * np.random.standard_normal(DIM)),
            "gk": bf(1.0 + 0.1 * np.random.standard_normal(DIM)),
            "freqs_cos": bf(np.cos(theta)),
            "freqs_sin": bf(np.sin(theta))}


def reference(x, wq, bq, wk, bk, gq, gk, freqs_cos, freqs_sin):
    xq = mxq(f64(x), 2, "e5m2")
    q = rmsnorm((xq @ mxq(f64(wq), 1, "e5m2").T) + f64(bq), f64(gq))
    k = rmsnorm((xq @ mxq(f64(wk), 1, "e5m2").T) + f64(bk), f64(gk))
    fc, fs = grid(f64(freqs_cos)), grid(f64(freqs_sin))
    return rope(q, fc, fs), rope(k, fc, fs)

@@ -1,0 +1,318 @@
+from contextlib import ExitStack
+
+import concourse.mybir as mybir
+from concourse.masks import make_identity
+
+S, K, DIM, HEADS = 1024, 1536, 1536, 12
+HEAD_DIM = DIM // HEADS
+EPS = 1e-6
+FLOPS = 2 * S * K * 2 * DIM
+
+F32 = mybir.dt.float32
+BF16 = mybir.dt.bfloat16
+U32 = mybir.dt.uint32
+U8 = mybir.dt.uint8
+E5M2X4 = mybir.dt.float8_e5m2_x4
+ACT = mybir.ActivationFunctionType
+ALU = mybir.AluOpType
+
+P = 128
+PASSES = K // 512
+UNIT = 256
+BANK = 512
+HEADS_PER_BANK = BANK // HEAD_DIM
+BANKS = DIM // BANK
+FRAMES, GRID_H, GRID_W = 4, 16, 16
+PAIRS = HEAD_DIM // 2
+F_PAIRS, H_PAIRS, W_PAIRS = 22, 21, 21
+F_COLS = 2 * F_PAIRS
+HW_COLS = HEAD_DIM - F_COLS
+TILES = S // P
+ROW_BIAS = GRID_H
+ROW_GAIN = ROW_BIAS + 2 * HEADS
+TOKEN_BANKS, ACC_BANKS = 5, 3
+BIG_BUFS = 6
+
+
+def tile_selfattention_pa_kernel(
+    tc, x, wq, bq, wk, bk, gq, gk, freqs_cos, freqs_sin, out_0, out_1
+):
+    nc = tc.nc
+    outs = [o.rearrange("b s h d -> (b s) (h d)") for o in (out_0, out_1)]
+
+    with ExitStack() as ctx:
+        keep = ctx.enter_context(tc.tile_pool(name="keep", bufs=1))
+        work = ctx.enter_context(tc.tile_pool(name="work", bufs=1))
+        psum = ctx.enter_context(tc.psum_pool(name="psum", bufs=1))
+        ctx.enter_context(tc.manual_schedule())
+
+        def token_bank(shape):
+            return psum.tile(shape, F32, name="token_bank", tag="token", bufs=TOKEN_BANKS)
+
+        def acc_bank(shape, dtype=F32):
+            return psum.tile(shape, dtype, name="acc_bank", tag="acc", bufs=ACC_BANKS)
+
+        def big_tile(shape, dtype):
+            return work.tile(shape, dtype, name="big", tag="big", bufs=BIG_BUFS)
+
+        x_codes = keep.tile([P, PASSES, S], U32, name="x_codes", align_bytes=64)
+        x_scales = keep.tile([P, PASSES, S], U8, name="x_scales", align_bytes=64)
+        w_codes = [keep.tile([P, PASSES, DIM], U32, name="w_codes%d" % j, align_bytes=64) for j in range(2)]
+        w_scales = [keep.tile([P, PASSES, DIM], U8, name="w_scales%d" % j, align_bytes=64) for j in range(2)]
+
+        x_rows = x.rearrange("b s k -> (b s) k")
+        units = []
+        for src, codes, scales in (
+            (wq, w_codes[0], w_scales[0]),
+            (x_rows, x_codes, x_scales),
+            (wk, w_codes[1], w_scales[1]),
+        ):
+            for r0 in range(0, src.shape[0], UNIT):
+                units.append((src, codes, scales, r0))
+
+        raw = {}
+
+        def load(u, column_pieces=1):
+            src, r0 = units[u][0], units[u][3]
+            raw[u] = big_tile([P, 2, K], BF16)
+            rows = src[r0 : r0 + UNIT, :].rearrange("(a p) k -> p a k", p=P)
+            width = K // column_pieces
+            for c0 in range(0, K, width):
+                nc.sync.dma_start(out=raw[u][:, :, c0 : c0 + width], in_=rows[:, :, c0 : c0 + width])
+
+        load(0, column_pieces=PASSES)
+        for u in range(1, BIG_BUFS - 1):
+            load(u)
+
+        ident = keep.tile([P, P], F32, name="ident")
+        make_identity(nc, ident[:])
+        small = keep.tile([P, P], BF16, name="small")
+        nc.vector.memset(small[:], 0.0)
+        nc.scalar.dma_start(out=small[0:GRID_H, 0:PAIRS], in_=freqs_cos[0:GRID_H, :])
+        nc.scalar.dma_start(out=small[0:GRID_H, PAIRS:P], in_=freqs_sin[0:GRID_H, :])
+        for j, (bias_vec, gain_vec) in enumerate(((bq, gq), (bk, gk))):
+            r = ROW_GAIN + HEADS * j
+            nc.scalar.dma_start(out=small[r : r + HEADS, :], in_=gain_vec.rearrange("(h d) -> h d", d=HEAD_DIM))
+            r = ROW_BIAS + HEADS * j
+            nc.gpsimd.dma_start(out=small[r : r + HEADS, :], in_=bias_vec.rearrange("(h d) -> h d", d=HEAD_DIM))
+
+        ident_bf = keep.tile([P, P], BF16, name="ident_bf")
+        nc.vector.tensor_copy(out=ident_bf[:], in_=ident[:])
+        signs = keep.tile([P, 2, 2], F32, name="signs")
+        nc.vector.memset(signs[:], 1.0)
+        nc.vector.memset(signs[:, 1, 1:2], -1.0)
+        pick_h = keep.tile([P, GRID_H, GRID_W], BF16, name="pick_h")
+        nc.vector.tensor_copy(
+            out=pick_h[:], in_=ident_bf[:, 0:GRID_H].unsqueeze(2).to_broadcast([P, GRID_H, GRID_W])
+        )
+        pick_w = keep.tile([P, P // GRID_W, GRID_W], BF16, name="pick_w")
+        nc.vector.tensor_copy(
+            out=pick_w[:], in_=ident_bf[:, 0:GRID_W].unsqueeze(1).to_broadcast([P, P // GRID_W, GRID_W])
+        )
+
+        def pick_row(r):
+            return ident_bf[:, r : r + 1].to_broadcast([P, P])
+
+        bias = keep.tile([P, 2 * HEADS], F32, name="bias")
+        angle_f = keep.tile([P, 2, FRAMES, F_PAIRS, 2], F32, name="angle_f")
+        angle_hw = keep.tile([P, 2, 2, H_PAIRS + W_PAIRS, 2], F32, name="angle_hw")
+
+        def spread_constants():
+            by_frame = acc_bank([P, FRAMES, P])
+            for f in range(FRAMES):
+                nc.tensor.matmul(by_frame[:, f, :], lhsT=pick_row(f), rhs=small[:], start=True, stop=True)
+            by_cell = acc_bank([P, 3, P])
+            pick_h_flat = pick_h[:].rearrange("r h w -> r (h w)")
+            for half in range(2):
+                nc.tensor.matmul(
+                    by_cell[:, half, :], lhsT=pick_h_flat[:, half * P : (half + 1) * P], rhs=small[:],
+                    start=True, stop=True,
+                )
+            nc.tensor.matmul(
+                by_cell[:, 2, :], lhsT=pick_w[:].rearrange("r h w -> r (h w)"), rhs=small[:], start=True, stop=True
+            )
+            small_t = acc_bank([P, P], BF16)
+            nc.tensor.transpose(small_t[:], small[:], ident_bf[:])
+
+            for kind in range(2):
+                c0 = kind * PAIRS
+                for out, src in (
+                    (angle_f[:, kind], by_frame[:, :, c0 : c0 + F_PAIRS]),
+                    (angle_hw[:, kind, :, 0:H_PAIRS, :], by_cell[:, 0:2, c0 + F_PAIRS : c0 + F_PAIRS + H_PAIRS]),
+                    (angle_hw[:, kind, :, H_PAIRS:, :], by_cell[:, 2:3, c0 + F_PAIRS + H_PAIRS : c0 + PAIRS]),
+                ):
+                    shape = list(out.shape)
+                    nc.vector.tensor_tensor(
+                        out=out,
+                        in0=src.unsqueeze(3).to_broadcast(shape),
+                        in1=signs[:, kind, :].unsqueeze(1).unsqueeze(1).to_broadcast(shape),
+                        op=ALU.mult,
+                    )
+            nc.vector.tensor_copy(out=bias[:], in_=small_t[:, ROW_BIAS:ROW_GAIN])
+
+        table_f = [keep.tile([P, 2, FRAMES, HEADS, F_COLS], F32, name="table_f%d" % j) for j in range(2)]
+        table_hw = [keep.tile([P, 2, 2, HEADS, HW_COLS], F32, name="table_hw%d" % j) for j in range(2)]
+        gains = {}
+
+        def spread_gains(n, bank):
+            j, b = divmod(n, BANKS)
+            gains[n] = bank([P, HEADS_PER_BANK, HEAD_DIM])
+            for i in range(HEADS_PER_BANK):
+                r = ROW_GAIN + HEADS * j + HEADS_PER_BANK * b + i
+                nc.tensor.matmul(gains[n][:, i, :], lhsT=pick_row(r), rhs=small[:], start=True, stop=True)
+
+        def table_step(t):
+            n, rest = divmod(t, 4)
+            kind, part = divmod(rest, 2)
+            j, b = divmod(n, BANKS)
+            heads = slice(HEADS_PER_BANK * b, HEADS_PER_BANK * (b + 1))
+            table, angle, cols = (
+                (table_f[j], angle_f, slice(0, F_COLS)),
+                (table_hw[j], angle_hw, slice(F_COLS, HEAD_DIM)),
+            )[part]
+            out = table[:, kind, :, heads, :]
+            shape = list(out.shape)
+            nc.vector.tensor_tensor(
+                out=out,
+                in0=gains[n][:, :, cols].unsqueeze(1).to_broadcast(shape),
+                in1=angle[:, kind].rearrange("p v j e -> p v (j e)").unsqueeze(2).to_broadcast(shape),
+                op=ALU.mult,
+            )
+
+        def quantize_unit(u):
+            codes, scales, r0 = units[u][1:]
+            words = raw[u][:].rearrange("p a k -> p (a k)").bitcast(F32)
+            for g in range(PASSES):
+                turned = token_bank([P, 2, 2, P])
+                for a in range(2):
+                    w0 = a * (K // 2) + g * 256
+                    for e in range(2):
+                        nc.tensor.transpose(turned[:, a, e, :], words[:, w0 + e : w0 + 256 : 2], ident[:])
+                grouped = work.tile([P, 4 * UNIT], BF16, name="grouped", bufs=4, align_bytes=64)
+                nc.scalar.copy(
+                    out=grouped[:].bitcast(F32).rearrange("p (a r e) -> p a r e", a=2, e=2),
+                    in_=turned[:].rearrange("p a e r -> p a r e"),
+                )
+                nc.vector.quantize_mx(
+                    out=codes[:, g, r0 : r0 + UNIT].bitcast(E5M2X4),
+                    scales=scales[:, g, r0 : r0 + UNIT],
+                    in_=grouped[:],
+                )
+
+        first_table_unit = 2
+        for u in range(len(units)):
+            if u + BIG_BUFS - 1 < len(units):
+                load(u + BIG_BUFS - 1)
+            t = u - first_table_unit
+            if t >= 0 and t % 4 == 0:
+                spread_gains(t // 4, acc_bank)
+            quantize_unit(u)
+            if t == -1:
+                spread_constants()
+            if t >= 0:
+                table_step(t)
+        tables_done = len(units) - first_table_unit
+        for n in range((tables_done + 3) // 4, 2 * BANKS):
+            spread_gains(n, token_bank)
+        for t in range(tables_done, 8 * BANKS):
+            table_step(t)
+
+        channel_major = {}
+        sums = {}
+
+        def project(c, j):
+            proj, frame = divmod(c // 2, FRAMES)
+            tokens = slice(frame * UNIT, (frame + 1) * UNIT)
+            sums[c, j] = acc_bank([P, 2, UNIT])
+            for i in range(2):
+                h = 6 * (c % 2) + 2 * j + i
+                chans = slice(h * HEAD_DIM, (h + 1) * HEAD_DIM)
+                for g in range(PASSES):
+                    nc.tensor.matmul_mx(
+                        out=sums[c, j][:, i, :],
+                        lhsT=w_codes[proj][:, g, chans].bitcast(E5M2X4),
+                        lhsT_scale=w_scales[proj][:, g, chans],
+                        rhs=x_codes[:, g, tokens].bitcast(E5M2X4),
+                        rhs_scale=x_scales[:, g, tokens],
+                        start=(g == 0),
+                        stop=(g == PASSES - 1),
+                    )
+
+        def add_bias(c, n):
+            group = c // 2
+            if group not in channel_major:
+                channel_major[group] = work.tile([P, HEADS, UNIT], F32, name="channel_major", bufs=2)
+            h = 6 * (c % 2) + n
+            col = HEADS * (group // FRAMES) + h
+            nc.scalar.activation(
+                out=channel_major[group][:, h, :], in_=sums[c, n // 2][:, n % 2, :],
+                func=ACT.Identity, bias=bias[:, col : col + 1],
+            )
+
+        chunks = 2 * TILES
+        for c in range(2):
+            for j in range(3):
+                project(c, j)
+                if (c, j) != (1, 2):
+                    add_bias(c, 2 * j)
+                    add_bias(c, 2 * j + 1)
+
+        for s in range(2 * TILES):
+            proj, tile_no = divmod(s, TILES)
+            frame, half = divmod(tile_no, 2)
+            if s + 1 < chunks:
+                add_bias(s + 1, 4)
+                add_bias(s + 1, 5)
+
+            token_major = []
+            stats = work.tile([P, 8], F32, name="stats", bufs=3)
+            for b in range(BANKS):
+                bank = token_bank([P, HEADS_PER_BANK, HEAD_DIM])
+                token_major.append(bank)
+                for i in range(HEADS_PER_BANK):
+                    h = HEADS_PER_BANK * b + i
+                    nc.tensor.transpose(
+                        bank[:, i, :], channel_major[s // 2][:, h, half * P : (half + 1) * P], ident[:]
+                    )
+                squares = work.tile([P, BANK], BF16, name="squares", bufs=2)
+                nc.scalar.activation(
+                    out=squares[:], in_=bank[:].rearrange("p h d -> p (h d)"), func=ACT.Square,
+                    accum_out=stats[:, b : b + 1],
+                )
+
+            more = s + 2 < chunks
+            if more:
+                for j in range(3):
+                    project(s + 2, j)
+            nc.scalar.activation(
+                out=stats[:, 3:6], in_=stats[:, 0:3], func=ACT.Identity, accum_out=stats[:, 6:7]
+            )
+            if more:
+                add_bias(s + 2, 0)
+            rstd = stats[:, 7:8]
+            nc.scalar.activation(
+                out=rstd, in_=stats[:, 6:7], func=ACT.Abs_reciprocal_sqrt, scale=1.0 / DIM, bias=EPS
+            )
+            if more:
+                for n in range(1, 4):
+                    add_bias(s + 2, n)
+
+            terms = [big_tile([P, HEADS, HEAD_DIM], F32) for kind in range(2)]
+            for b in range(BANKS):
+                heads = slice(HEADS_PER_BANK * b, HEADS_PER_BANK * (b + 1))
+                for kind in range(2):
+                    for cols, table in (
+                        (slice(0, F_COLS), table_f[proj][:, kind, frame, heads, :]),
+                        (slice(F_COLS, HEAD_DIM), table_hw[proj][:, kind, half, heads, :]),
+                    ):
+                        nc.vector.scalar_tensor_tensor(
+                            out=terms[kind][:, heads, cols], in0=token_major[b][:, :, cols], scalar=rstd,
+                            in1=table, op0=ALU.mult, op1=ALU.mult,
+                        )
+                cos_term = terms[0][:, heads, :].rearrange("p h (j e) -> p (h j) e", e=2)
+                sin_term = terms[1][:, heads, :].rearrange("p h (j e) -> p (h j) e", e=2)
+                nc.gpsimd.tensor_tensor(out=cos_term, in0=cos_term, in1=sin_term[:, :, ::-1], op=ALU.add)
+                nc.sync.dma_start(
+                    out=outs[proj][tile_no * P : (tile_no + 1) * P, b * BANK : (b + 1) * BANK],
+                    in_=terms[0][:, heads, :].rearrange("p h d -> p (h d)"),
+                )

@@ -28,10 +28,13 @@ F_PAIRS, H_PAIRS, W_PAIRS = 22, 21, 21
 F_COLS = 2 * F_PAIRS
 HW_COLS = HEAD_DIM - F_COLS
 TILES = S // P
-ROW_BIAS = GRID_H
-ROW_GAIN = ROW_BIAS + 2 * HEADS
 TOKEN_BANKS, ACC_BANKS = 5, 3
 BIG_BUFS = 6
+QUANT_BANKS = 4
+CONST_UNIT = 0
+BIAS_UNIT = 4
+TABLE_UNITS = (1, 2, 4, 5, 7, 8, 10, 11)
+ADD_AFTER = (1, 2)
 
 
 def tile_selfattention_pa_kernel(
@@ -55,25 +58,21 @@ def tile_selfattention_pa_kernel(
         def big_tile(shape, dtype):
             return work.tile(shape, dtype, name="big", tag="big", bufs=BIG_BUFS)
 
-        x_codes = keep.tile([P, PASSES, S], U32, name="x_codes", align_bytes=64)
-        x_scales = keep.tile([P, PASSES, S], U8, name="x_scales", align_bytes=64)
-        w_codes = [keep.tile([P, PASSES, DIM], U32, name="w_codes%d" % j, align_bytes=64) for j in range(2)]
-        w_scales = [keep.tile([P, PASSES, DIM], U8, name="w_scales%d" % j, align_bytes=64) for j in range(2)]
-
         x_rows = x.rearrange("b s k -> (b s) k")
-        units = []
-        for src, codes, scales in (
-            (wq, w_codes[0], w_scales[0]),
-            (x_rows, x_codes, x_scales),
-            (wk, w_codes[1], w_scales[1]),
-        ):
-            for r0 in range(0, src.shape[0], UNIT):
-                units.append((src, codes, scales, r0))
+        units = [(src, r0) for src in (wq, x_rows, wk) for r0 in range(0, src.shape[0], UNIT)]
+        first_x_unit = DIM // UNIT
+        first_w_unit = (0, first_x_unit + S // UNIT)
+        codes = keep.tile([P, len(units) * PASSES * UNIT], U32, name="codes", align_bytes=64)
+        scales = keep.tile([P, len(units) * PASSES * UNIT], U8, name="scales", align_bytes=64)
+
+        def operand(u, g, r0, rows):
+            c0 = (u * PASSES + g) * UNIT + r0
+            return codes[:, c0 : c0 + rows].bitcast(E5M2X4), scales[:, c0 : c0 + rows]
 
         raw = {}
 
         def load(u, column_pieces=1):
-            src, r0 = units[u][0], units[u][3]
+            src, r0 = units[u]
             raw[u] = big_tile([P, 2, K], BF16)
             rows = src[r0 : r0 + UNIT, :].rearrange("(a p) k -> p a k", p=P)
             width = K // column_pieces
@@ -81,20 +80,24 @@ def tile_selfattention_pa_kernel(
                 nc.sync.dma_start(out=raw[u][:, :, c0 : c0 + width], in_=rows[:, :, c0 : c0 + width])
 
         load(0, column_pieces=PASSES)
-        for u in range(1, BIG_BUFS - 1):
-            load(u)
-
+        early = keep.tile([P, P], BF16, name="early")
+        later = keep.tile([P, P], BF16, name="later")
+        nc.vector.memset(early[:], 0.0)
+        nc.vector.memset(later[:], 0.0)
         ident = keep.tile([P, P], F32, name="ident")
         make_identity(nc, ident[:])
-        small = keep.tile([P, P], BF16, name="small")
-        nc.vector.memset(small[:], 0.0)
-        nc.scalar.dma_start(out=small[0:GRID_H, 0:PAIRS], in_=freqs_cos[0:GRID_H, :])
-        nc.scalar.dma_start(out=small[0:GRID_H, PAIRS:P], in_=freqs_sin[0:GRID_H, :])
-        for j, (bias_vec, gain_vec) in enumerate(((bq, gq), (bk, gk))):
-            r = ROW_GAIN + HEADS * j
-            nc.scalar.dma_start(out=small[r : r + HEADS, :], in_=gain_vec.rearrange("(h d) -> h d", d=HEAD_DIM))
-            r = ROW_BIAS + HEADS * j
-            nc.gpsimd.dma_start(out=small[r : r + HEADS, :], in_=bias_vec.rearrange("(h d) -> h d", d=HEAD_DIM))
+
+        def load_by_head(queue, rows, r, vec):
+            queue.dma_start(out=rows[r : r + HEADS, :], in_=vec.rearrange("(h d) -> h d", d=HEAD_DIM))
+
+        nc.sync.dma_start(out=early[0:GRID_H, 0:PAIRS], in_=freqs_cos[0:GRID_H, :])
+        nc.sync.dma_start(out=early[0:GRID_H, PAIRS:P], in_=freqs_sin[0:GRID_H, :])
+        load_by_head(nc.sync, early, GRID_H, gq)
+        for j, vec in enumerate((gk, bq, bk)):
+            load_by_head(nc.gpsimd, later, HEADS * j, vec)
+        gain_rows = ((early, GRID_H), (later, 0))
+        for u in range(1, BIG_BUFS - 1):
+            load(u)
 
         ident_bf = keep.tile([P, P], BF16, name="ident_bf")
         nc.vector.tensor_copy(out=ident_bf[:], in_=ident[:])
@@ -120,19 +123,17 @@ def tile_selfattention_pa_kernel(
         def spread_constants():
             by_frame = acc_bank([P, FRAMES, P])
             for f in range(FRAMES):
-                nc.tensor.matmul(by_frame[:, f, :], lhsT=pick_row(f), rhs=small[:], start=True, stop=True)
+                nc.tensor.matmul(by_frame[:, f, :], lhsT=pick_row(f), rhs=early[:], start=True, stop=True)
             by_cell = acc_bank([P, 3, P])
             pick_h_flat = pick_h[:].rearrange("r h w -> r (h w)")
             for half in range(2):
                 nc.tensor.matmul(
-                    by_cell[:, half, :], lhsT=pick_h_flat[:, half * P : (half + 1) * P], rhs=small[:],
+                    by_cell[:, half, :], lhsT=pick_h_flat[:, half * P : (half + 1) * P], rhs=early[:],
                     start=True, stop=True,
                 )
             nc.tensor.matmul(
-                by_cell[:, 2, :], lhsT=pick_w[:].rearrange("r h w -> r (h w)"), rhs=small[:], start=True, stop=True
+                by_cell[:, 2, :], lhsT=pick_w[:].rearrange("r h w -> r (h w)"), rhs=early[:], start=True, stop=True
             )
-            small_t = acc_bank([P, P], BF16)
-            nc.tensor.transpose(small_t[:], small[:], ident_bf[:])
 
             for kind in range(2):
                 c0 = kind * PAIRS
@@ -148,7 +149,11 @@ def tile_selfattention_pa_kernel(
                         in1=signs[:, kind, :].unsqueeze(1).unsqueeze(1).to_broadcast(shape),
                         op=ALU.mult,
                     )
-            nc.vector.tensor_copy(out=bias[:], in_=small_t[:, ROW_BIAS:ROW_GAIN])
+
+        def turn_biases():
+            later_t = acc_bank([P, P], BF16)
+            nc.tensor.transpose(later_t[:], later[:], ident_bf[:])
+            nc.vector.tensor_copy(out=bias[:], in_=later_t[:, HEADS : 3 * HEADS])
 
         table_f = [keep.tile([P, 2, FRAMES, HEADS, F_COLS], F32, name="table_f%d" % j) for j in range(2)]
         table_hw = [keep.tile([P, 2, 2, HEADS, HW_COLS], F32, name="table_hw%d" % j) for j in range(2)]
@@ -158,29 +163,30 @@ def tile_selfattention_pa_kernel(
             j, b = divmod(n, BANKS)
             gains[n] = bank([P, HEADS_PER_BANK, HEAD_DIM])
             for i in range(HEADS_PER_BANK):
-                r = ROW_GAIN + HEADS * j + HEADS_PER_BANK * b + i
-                nc.tensor.matmul(gains[n][:, i, :], lhsT=pick_row(r), rhs=small[:], start=True, stop=True)
+                rows, r0 = gain_rows[j]
+                r = r0 + HEADS_PER_BANK * b + i
+                nc.tensor.matmul(gains[n][:, i, :], lhsT=pick_row(r), rhs=rows[:], start=True, stop=True)
 
         def table_step(t):
-            n, rest = divmod(t, 4)
-            kind, part = divmod(rest, 2)
+            n, part = divmod(t, 2)
             j, b = divmod(n, BANKS)
             heads = slice(HEADS_PER_BANK * b, HEADS_PER_BANK * (b + 1))
             table, angle, cols = (
                 (table_f[j], angle_f, slice(0, F_COLS)),
                 (table_hw[j], angle_hw, slice(F_COLS, HEAD_DIM)),
             )[part]
-            out = table[:, kind, :, heads, :]
+            out = table[:, :, :, heads, :].rearrange("p k v h c -> p (k v) h c")
             shape = list(out.shape)
             nc.vector.tensor_tensor(
                 out=out,
                 in0=gains[n][:, :, cols].unsqueeze(1).to_broadcast(shape),
-                in1=angle[:, kind].rearrange("p v j e -> p v (j e)").unsqueeze(2).to_broadcast(shape),
+                in1=angle[:].rearrange("p k v j e -> p (k v) (j e)").unsqueeze(2).to_broadcast(shape),
                 op=ALU.mult,
             )
 
+        grouped = {}
+
         def quantize_unit(u):
-            codes, scales, r0 = units[u][1:]
             words = raw[u][:].rearrange("p a k -> p (a k)").bitcast(F32)
             for g in range(PASSES):
                 turned = token_bank([P, 2, 2, P])
@@ -188,33 +194,40 @@ def tile_selfattention_pa_kernel(
                     w0 = a * (K // 2) + g * 256
                     for e in range(2):
                         nc.tensor.transpose(turned[:, a, e, :], words[:, w0 + e : w0 + 256 : 2], ident[:])
-                grouped = work.tile([P, 4 * UNIT], BF16, name="grouped", bufs=4, align_bytes=64)
+                batch, slot = divmod(u * PASSES + g, QUANT_BANKS)
+                if slot == 0:
+                    grouped[batch] = work.tile(
+                        [P, QUANT_BANKS * 4 * UNIT], BF16, name="grouped", bufs=3, align_bytes=64
+                    )
                 nc.scalar.copy(
-                    out=grouped[:].bitcast(F32).rearrange("p (a r e) -> p a r e", a=2, e=2),
+                    out=grouped[batch][:].bitcast(F32)[:, slot * BANK : (slot + 1) * BANK].rearrange(
+                        "p (a r e) -> p a r e", a=2, e=2
+                    ),
                     in_=turned[:].rearrange("p a e r -> p a r e"),
                 )
-                nc.vector.quantize_mx(
-                    out=codes[:, g, r0 : r0 + UNIT].bitcast(E5M2X4),
-                    scales=scales[:, g, r0 : r0 + UNIT],
-                    in_=grouped[:],
-                )
+                if slot == QUANT_BANKS - 1:
+                    cols = slice(batch * QUANT_BANKS * UNIT, (batch + 1) * QUANT_BANKS * UNIT)
+                    nc.vector.quantize_mx(
+                        out=codes[:, cols].bitcast(E5M2X4), scales=scales[:, cols], in_=grouped[batch][:]
+                    )
 
-        first_table_unit = 2
         for u in range(len(units)):
             if u + BIG_BUFS - 1 < len(units):
                 load(u + BIG_BUFS - 1)
-            t = u - first_table_unit
-            if t >= 0 and t % 4 == 0:
-                spread_gains(t // 4, acc_bank)
+            t = TABLE_UNITS.index(u) if u in TABLE_UNITS else -1
+            if t >= 0 and t % 2 == 0:
+                spread_gains(t // 2, acc_bank)
             quantize_unit(u)
-            if t == -1:
+            if u == CONST_UNIT:
                 spread_constants()
+            if u == BIAS_UNIT:
+                turn_biases()
             if t >= 0:
                 table_step(t)
-        tables_done = len(units) - first_table_unit
-        for n in range((tables_done + 3) // 4, 2 * BANKS):
+        tables_done = len(TABLE_UNITS)
+        for n in range((tables_done + 1) // 2, 2 * BANKS):
             spread_gains(n, token_bank)
-        for t in range(tables_done, 8 * BANKS):
+        for t in range(tables_done, 4 * BANKS):
             table_step(t)
 
         channel_major = {}
@@ -222,18 +235,18 @@ def tile_selfattention_pa_kernel(
 
         def project(c, j):
             proj, frame = divmod(c // 2, FRAMES)
-            tokens = slice(frame * UNIT, (frame + 1) * UNIT)
             sums[c, j] = acc_bank([P, 2, UNIT])
             for i in range(2):
                 h = 6 * (c % 2) + 2 * j + i
-                chans = slice(h * HEAD_DIM, (h + 1) * HEAD_DIM)
                 for g in range(PASSES):
+                    w_codes, w_scales = operand(first_w_unit[proj] + h // 2, g, (h % 2) * HEAD_DIM, HEAD_DIM)
+                    x_codes, x_scales = operand(first_x_unit + frame, g, 0, UNIT)
                     nc.tensor.matmul_mx(
                         out=sums[c, j][:, i, :],
-                        lhsT=w_codes[proj][:, g, chans].bitcast(E5M2X4),
-                        lhsT_scale=w_scales[proj][:, g, chans],
-                        rhs=x_codes[:, g, tokens].bitcast(E5M2X4),
-                        rhs_scale=x_scales[:, g, tokens],
+                        lhsT=w_codes,
+                        lhsT_scale=w_scales,
+                        rhs=x_codes,
+                        rhs_scale=x_scales,
                         start=(g == 0),
                         stop=(g == PASSES - 1),
                     )
@@ -247,6 +260,15 @@ def tile_selfattention_pa_kernel(
             nc.scalar.activation(
                 out=channel_major[group][:, h, :], in_=sums[c, n // 2][:, n % 2, :],
                 func=ACT.Identity, bias=bias[:, col : col + 1],
+            )
+
+        def finish(engine, terms, heads, out, tile_no):
+            cos_term = terms[0][:, heads, :].rearrange("p h (j e) -> p (h j) e", e=2)
+            sin_term = terms[1][:, heads, :].rearrange("p h (j e) -> p (h j) e", e=2)
+            engine.tensor_tensor(out=cos_term, in0=cos_term, in1=sin_term[:, :, ::-1], op=ALU.add)
+            nc.sync.dma_start(
+                out=out[tile_no * P : (tile_no + 1) * P, heads.start * HEAD_DIM : heads.stop * HEAD_DIM],
+                in_=terms[0][:, heads, :].rearrange("p h d -> p (h d)"),
             )
 
         chunks = 2 * TILES
@@ -279,25 +301,28 @@ def tile_selfattention_pa_kernel(
                     out=squares[:], in_=bank[:].rearrange("p h d -> p (h d)"), func=ACT.Square,
                     accum_out=stats[:, b : b + 1],
                 )
+                if b == BANKS - 1:
+                    nc.scalar.activation(
+                        out=stats[:, 3:5], in_=stats[:, 0:2], func=ACT.Identity, scale=1.0 / DIM, bias=EPS / 2,
+                        accum_out=stats[:, 6:7],
+                    )
 
             more = s + 2 < chunks
             if more:
                 for j in range(3):
                     project(s + 2, j)
-            nc.scalar.activation(
-                out=stats[:, 3:6], in_=stats[:, 0:3], func=ACT.Identity, accum_out=stats[:, 6:7]
-            )
-            if more:
                 add_bias(s + 2, 0)
             rstd = stats[:, 7:8]
             nc.scalar.activation(
-                out=rstd, in_=stats[:, 6:7], func=ACT.Abs_reciprocal_sqrt, scale=1.0 / DIM, bias=EPS
+                out=rstd, in_=stats[:, 2:3], func=ACT.Abs_reciprocal_sqrt, scale=1.0 / DIM, bias=stats[:, 6:7]
             )
             if more:
                 for n in range(1, 4):
                     add_bias(s + 2, n)
 
             terms = [big_tile([P, HEADS, HEAD_DIM], F32) for kind in range(2)]
+            pending = []
+            added = 0
             for b in range(BANKS):
                 heads = slice(HEADS_PER_BANK * b, HEADS_PER_BANK * (b + 1))
                 for kind in range(2):
@@ -309,10 +334,11 @@ def tile_selfattention_pa_kernel(
                             out=terms[kind][:, heads, cols], in0=token_major[b][:, :, cols], scalar=rstd,
                             in1=table, op0=ALU.mult, op1=ALU.mult,
                         )
-                cos_term = terms[0][:, heads, :].rearrange("p h (j e) -> p (h j) e", e=2)
-                sin_term = terms[1][:, heads, :].rearrange("p h (j e) -> p (h j) e", e=2)
-                nc.gpsimd.tensor_tensor(out=cos_term, in0=cos_term, in1=sin_term[:, :, ::-1], op=ALU.add)
-                nc.sync.dma_start(
-                    out=outs[proj][tile_no * P : (tile_no + 1) * P, b * BANK : (b + 1) * BANK],
-                    in_=terms[0][:, heads, :].rearrange("p h d -> p (h d)"),
-                )
+                last = s == 2 * TILES - 1
+                if last or b in ADD_AFTER:
+                    pending.append(slice(added, heads.stop))
+                    added = heads.stop
+                    if not last or b == 0:
+                        finish(nc.gpsimd, terms, pending.pop(), outs[proj], tile_no)
+            for done in pending:
+                finish(nc.vector, terms, done, outs[proj], tile_no)

@@ -33,6 +33,7 @@ BIG_BUFS = 6
 QUANT_BANKS = 4
 CONST_UNIT = 0
 BIAS_UNIT = 4
+GAIN_UNITS = (1, 4, 7, 10, 12, 14)
 TABLE_UNITS = (1, 2, 4, 5, 7, 8, 10, 11)
 ADD_AFTER = (1, 2)
 
@@ -74,7 +75,7 @@ def tile_selfattention_pa_kernel(
         def load(u, column_pieces=1):
             src, r0 = units[u]
             raw[u] = big_tile([P, 2, K], BF16)
-            rows = src[r0 : r0 + UNIT, :].rearrange("(a p) k -> p a k", p=P)
+            rows = src[r0 : r0 + UNIT, :].rearrange("(p a) k -> p a k", a=2)
             width = K // column_pieces
             for c0 in range(0, K, width):
                 nc.sync.dma_start(out=raw[u][:, :, c0 : c0 + width], in_=rows[:, :, c0 : c0 + width])
@@ -201,9 +202,9 @@ def tile_selfattention_pa_kernel(
                     )
                 nc.scalar.copy(
                     out=grouped[batch][:].bitcast(F32)[:, slot * BANK : (slot + 1) * BANK].rearrange(
-                        "p (a r e) -> p a r e", a=2, e=2
+                        "p (r a e) -> p r a e", a=2, e=2
                     ),
-                    in_=turned[:].rearrange("p a e r -> p a r e"),
+                    in_=turned[:].rearrange("p a e r -> p r a e"),
                 )
                 if slot == QUANT_BANKS - 1:
                     cols = slice(batch * QUANT_BANKS * UNIT, (batch + 1) * QUANT_BANKS * UNIT)
@@ -215,8 +216,8 @@ def tile_selfattention_pa_kernel(
             if u + BIG_BUFS - 1 < len(units):
                 load(u + BIG_BUFS - 1)
             t = TABLE_UNITS.index(u) if u in TABLE_UNITS else -1
-            if t >= 0 and t % 2 == 0:
-                spread_gains(t // 2, acc_bank)
+            if u in GAIN_UNITS:
+                spread_gains(GAIN_UNITS.index(u), acc_bank)
             quantize_unit(u)
             if u == CONST_UNIT:
                 spread_constants()
@@ -225,17 +226,15 @@ def tile_selfattention_pa_kernel(
             if t >= 0:
                 table_step(t)
         tables_done = len(TABLE_UNITS)
-        for n in range((tables_done + 1) // 2, 2 * BANKS):
-            spread_gains(n, token_bank)
         for t in range(tables_done, 4 * BANKS):
             table_step(t)
 
         channel_major = {}
         sums = {}
 
-        def project(c, j):
+        def project(c, j, bank):
             proj, frame = divmod(c // 2, FRAMES)
-            sums[c, j] = acc_bank([P, 2, UNIT])
+            sums[c, j] = bank([P, 2, UNIT])
             for i in range(2):
                 h = 6 * (c % 2) + 2 * j + i
                 for g in range(PASSES):
@@ -274,7 +273,7 @@ def tile_selfattention_pa_kernel(
         chunks = 2 * TILES
         for c in range(2):
             for j in range(3):
-                project(c, j)
+                project(c, j, token_bank)
                 if (c, j) != (1, 2):
                     add_bias(c, 2 * j)
                     add_bias(c, 2 * j + 1)
@@ -310,7 +309,7 @@ def tile_selfattention_pa_kernel(
             more = s + 2 < chunks
             if more:
                 for j in range(3):
-                    project(s + 2, j)
+                    project(s + 2, j, acc_bank)
                 add_bias(s + 2, 0)
             rstd = stats[:, 7:8]
             nc.scalar.activation(

@@ -105,6 +105,8 @@ def tile_selfattention_pa_kernel(
         signs = keep.tile([P, 2, 2], F32, name="signs")
         nc.vector.memset(signs[:], 1.0)
         nc.vector.memset(signs[:, 1, 1:2], -1.0)
+        warm = keep.tile([P, 1], F32, name="warm")
+        nc.scalar.activation(out=warm[:], in_=signs[:, 0, 0:1], func=ACT.Abs_reciprocal_sqrt)
         pick_h = keep.tile([P, GRID_H, GRID_W], BF16, name="pick_h")
         nc.vector.tensor_copy(
             out=pick_h[:], in_=ident_bf[:, 0:GRID_H].unsqueeze(2).to_broadcast([P, GRID_H, GRID_W])

from contextlib import ExitStack

import concourse.mybir as mybir
from concourse.masks import make_identity

S, K, DIM, HEADS = 1024, 1536, 1536, 12
HEAD_DIM = DIM // HEADS
EPS = 1e-6
FLOPS = 2 * S * K * 2 * DIM

F32 = mybir.dt.float32
BF16 = mybir.dt.bfloat16
U32 = mybir.dt.uint32
U8 = mybir.dt.uint8
E5M2X4 = mybir.dt.float8_e5m2_x4
ACT = mybir.ActivationFunctionType
ALU = mybir.AluOpType

P = 128
PASSES = K // 512
UNIT = 256
BANK = 512
HEADS_PER_BANK = BANK // HEAD_DIM
BANKS = DIM // BANK
FRAMES, GRID_H, GRID_W = 4, 16, 16
PAIRS = HEAD_DIM // 2
F_PAIRS, H_PAIRS, W_PAIRS = 22, 21, 21
F_COLS = 2 * F_PAIRS
HW_COLS = HEAD_DIM - F_COLS
TILES = S // P
TOKEN_BANKS, ACC_BANKS = 5, 3
BIG_BUFS = 6
QUANT_BANKS = 4
CONST_UNIT = 0
BIAS_UNIT = 4
GAIN_UNITS = (1, 4, 7, 10, 12, 14)
TABLE_UNITS = (1, 2, 4, 5, 7, 8, 10, 11)
ADD_AFTER = (1, 2)


def tile_selfattention_pa_kernel(
    tc, x, wq, bq, wk, bk, gq, gk, freqs_cos, freqs_sin, out_0, out_1
):
    nc = tc.nc
    outs = [o.rearrange("b s h d -> (b s) (h d)") for o in (out_0, out_1)]

    with ExitStack() as ctx:
        keep = ctx.enter_context(tc.tile_pool(name="keep", bufs=1))
        work = ctx.enter_context(tc.tile_pool(name="work", bufs=1))
        psum = ctx.enter_context(tc.psum_pool(name="psum", bufs=1))
        ctx.enter_context(tc.manual_schedule())

        def token_bank(shape):
            return psum.tile(shape, F32, name="token_bank", tag="token", bufs=TOKEN_BANKS)

        def acc_bank(shape, dtype=F32):
            return psum.tile(shape, dtype, name="acc_bank", tag="acc", bufs=ACC_BANKS)

        def big_tile(shape, dtype):
            return work.tile(shape, dtype, name="big", tag="big", bufs=BIG_BUFS)

        x_rows = x.rearrange("b s k -> (b s) k")
        units = [(src, r0) for src in (wq, x_rows, wk) for r0 in range(0, src.shape[0], UNIT)]
        first_x_unit = DIM // UNIT
        first_w_unit = (0, first_x_unit + S // UNIT)
        codes = keep.tile([P, len(units) * PASSES * UNIT], U32, name="codes", align_bytes=64)
        scales = keep.tile([P, len(units) * PASSES * UNIT], U8, name="scales", align_bytes=64)

        def operand(u, g, r0, rows):
            c0 = (u * PASSES + g) * UNIT + r0
            return codes[:, c0 : c0 + rows].bitcast(E5M2X4), scales[:, c0 : c0 + rows]

        raw = {}

        def load(u, column_pieces=1):
            src, r0 = units[u]
            raw[u] = big_tile([P, 2, K], BF16)
            rows = src[r0 : r0 + UNIT, :].rearrange("(p a) k -> p a k", a=2)
            width = K // column_pieces
            for c0 in range(0, K, width):
                nc.sync.dma_start(out=raw[u][:, :, c0 : c0 + width], in_=rows[:, :, c0 : c0 + width])

        load(0, column_pieces=PASSES)
        early = keep.tile([P, P], BF16, name="early")
        later = keep.tile([P, P], BF16, name="later")
        nc.vector.memset(early[:], 0.0)
        nc.vector.memset(later[:], 0.0)
        ident = keep.tile([P, P], F32, name="ident")
        make_identity(nc, ident[:])

        def load_by_head(queue, rows, r, vec):
            queue.dma_start(out=rows[r : r + HEADS, :], in_=vec.rearrange("(h d) -> h d", d=HEAD_DIM))

        nc.sync.dma_start(out=early[0:GRID_H, 0:PAIRS], in_=freqs_cos[0:GRID_H, :])
        nc.sync.dma_start(out=early[0:GRID_H, PAIRS:P], in_=freqs_sin[0:GRID_H, :])
        load_by_head(nc.sync, early, GRID_H, gq)
        for j, vec in enumerate((gk, bq, bk)):
            load_by_head(nc.gpsimd, later, HEADS * j, vec)
        gain_rows = ((early, GRID_H), (later, 0))
        for u in range(1, BIG_BUFS - 1):
            load(u)

        ident_bf = keep.tile([P, P], BF16, name="ident_bf")
        nc.vector.tensor_copy(out=ident_bf[:], in_=ident[:])
        signs = keep.tile([P, 2, 2], F32, name="signs")
        nc.vector.memset(signs[:], 1.0)
        nc.vector.memset(signs[:, 1, 1:2], -1.0)
        warm = keep.tile([P, 1], F32, name="warm")
        nc.scalar.activation(out=warm[:], in_=signs[:, 0, 0:1], func=ACT.Abs_reciprocal_sqrt)
        pick_h = keep.tile([P, GRID_H, GRID_W], BF16, name="pick_h")
        nc.vector.tensor_copy(
            out=pick_h[:], in_=ident_bf[:, 0:GRID_H].unsqueeze(2).to_broadcast([P, GRID_H, GRID_W])
        )
        pick_w = keep.tile([P, P // GRID_W, GRID_W], BF16, name="pick_w")
        nc.vector.tensor_copy(
            out=pick_w[:], in_=ident_bf[:, 0:GRID_W].unsqueeze(1).to_broadcast([P, P // GRID_W, GRID_W])
        )

        def pick_row(r):
            return ident_bf[:, r : r + 1].to_broadcast([P, P])

        bias = keep.tile([P, 2 * HEADS], F32, name="bias")
        angle_f = keep.tile([P, 2, FRAMES, F_PAIRS, 2], F32, name="angle_f")
        angle_hw = keep.tile([P, 2, 2, H_PAIRS + W_PAIRS, 2], F32, name="angle_hw")

        def spread_constants():
            by_frame = acc_bank([P, FRAMES, P])
            for f in range(FRAMES):
                nc.tensor.matmul(by_frame[:, f, :], lhsT=pick_row(f), rhs=early[:], start=True, stop=True)
            by_cell = acc_bank([P, 3, P])
            pick_h_flat = pick_h[:].rearrange("r h w -> r (h w)")
            for half in range(2):
                nc.tensor.matmul(
                    by_cell[:, half, :], lhsT=pick_h_flat[:, half * P : (half + 1) * P], rhs=early[:],
                    start=True, stop=True,
                )
            nc.tensor.matmul(
                by_cell[:, 2, :], lhsT=pick_w[:].rearrange("r h w -> r (h w)"), rhs=early[:], start=True, stop=True
            )

            for kind in range(2):
                c0 = kind * PAIRS
                for out, src in (
                    (angle_f[:, kind], by_frame[:, :, c0 : c0 + F_PAIRS]),
                    (angle_hw[:, kind, :, 0:H_PAIRS, :], by_cell[:, 0:2, c0 + F_PAIRS : c0 + F_PAIRS + H_PAIRS]),
                    (angle_hw[:, kind, :, H_PAIRS:, :], by_cell[:, 2:3, c0 + F_PAIRS + H_PAIRS : c0 + PAIRS]),
                ):
                    shape = list(out.shape)
                    nc.vector.tensor_tensor(
                        out=out,
                        in0=src.unsqueeze(3).to_broadcast(shape),
                        in1=signs[:, kind, :].unsqueeze(1).unsqueeze(1).to_broadcast(shape),
                        op=ALU.mult,
                    )

        def turn_biases():
            later_t = acc_bank([P, P], BF16)
            nc.tensor.transpose(later_t[:], later[:], ident_bf[:])
            nc.vector.tensor_copy(out=bias[:], in_=later_t[:, HEADS : 3 * HEADS])

        table_f = [keep.tile([P, 2, FRAMES, HEADS, F_COLS], F32, name="table_f%d" % j) for j in range(2)]
        table_hw = [keep.tile([P, 2, 2, HEADS, HW_COLS], F32, name="table_hw%d" % j) for j in range(2)]
        gains = {}

        def spread_gains(n, bank):
            j, b = divmod(n, BANKS)
            gains[n] = bank([P, HEADS_PER_BANK, HEAD_DIM])
            for i in range(HEADS_PER_BANK):
                rows, r0 = gain_rows[j]
                r = r0 + HEADS_PER_BANK * b + i
                nc.tensor.matmul(gains[n][:, i, :], lhsT=pick_row(r), rhs=rows[:], start=True, stop=True)

        def table_step(t):
            n, part = divmod(t, 2)
            j, b = divmod(n, BANKS)
            heads = slice(HEADS_PER_BANK * b, HEADS_PER_BANK * (b + 1))
            table, angle, cols = (
                (table_f[j], angle_f, slice(0, F_COLS)),
                (table_hw[j], angle_hw, slice(F_COLS, HEAD_DIM)),
            )[part]
            out = table[:, :, :, heads, :].rearrange("p k v h c -> p (k v) h c")
            shape = list(out.shape)
            nc.vector.tensor_tensor(
                out=out,
                in0=gains[n][:, :, cols].unsqueeze(1).to_broadcast(shape),
                in1=angle[:].rearrange("p k v j e -> p (k v) (j e)").unsqueeze(2).to_broadcast(shape),
                op=ALU.mult,
            )

        grouped = {}

        def quantize_unit(u):
            words = raw[u][:].rearrange("p a k -> p (a k)").bitcast(F32)
            for g in range(PASSES):
                turned = token_bank([P, 2, 2, P])
                for a in range(2):
                    w0 = a * (K // 2) + g * 256
                    for e in range(2):
                        nc.tensor.transpose(turned[:, a, e, :], words[:, w0 + e : w0 + 256 : 2], ident[:])
                batch, slot = divmod(u * PASSES + g, QUANT_BANKS)
                if slot == 0:
                    grouped[batch] = work.tile(
                        [P, QUANT_BANKS * 4 * UNIT], BF16, name="grouped", bufs=3, align_bytes=64
                    )
                nc.scalar.copy(
                    out=grouped[batch][:].bitcast(F32)[:, slot * BANK : (slot + 1) * BANK].rearrange(
                        "p (r a e) -> p r a e", a=2, e=2
                    ),
                    in_=turned[:].rearrange("p a e r -> p r a e"),
                )
                if slot == QUANT_BANKS - 1:
                    cols = slice(batch * QUANT_BANKS * UNIT, (batch + 1) * QUANT_BANKS * UNIT)
                    nc.vector.quantize_mx(
                        out=codes[:, cols].bitcast(E5M2X4), scales=scales[:, cols], in_=grouped[batch][:]
                    )

        for u in range(len(units)):
            if u + BIG_BUFS - 1 < len(units):
                load(u + BIG_BUFS - 1)
            t = TABLE_UNITS.index(u) if u in TABLE_UNITS else -1
            if u in GAIN_UNITS:
                spread_gains(GAIN_UNITS.index(u), acc_bank)
            quantize_unit(u)
            if u == CONST_UNIT:
                spread_constants()
            if u == BIAS_UNIT:
                turn_biases()
            if t >= 0:
                table_step(t)
        tables_done = len(TABLE_UNITS)
        for t in range(tables_done, 4 * BANKS):
            table_step(t)

        channel_major = {}
        sums = {}

        def project(c, j, bank):
            proj, frame = divmod(c // 2, FRAMES)
            sums[c, j] = bank([P, 2, UNIT])
            for i in range(2):
                h = 6 * (c % 2) + 2 * j + i
                for g in range(PASSES):
                    w_codes, w_scales = operand(first_w_unit[proj] + h // 2, g, (h % 2) * HEAD_DIM, HEAD_DIM)
                    x_codes, x_scales = operand(first_x_unit + frame, g, 0, UNIT)
                    nc.tensor.matmul_mx(
                        out=sums[c, j][:, i, :],
                        lhsT=w_codes,
                        lhsT_scale=w_scales,
                        rhs=x_codes,
                        rhs_scale=x_scales,
                        start=(g == 0),
                        stop=(g == PASSES - 1),
                    )

        def add_bias(c, n):
            group = c // 2
            if group not in channel_major:
                channel_major[group] = work.tile([P, HEADS, UNIT], F32, name="channel_major", bufs=2)
            h = 6 * (c % 2) + n
            col = HEADS * (group // FRAMES) + h
            nc.scalar.activation(
                out=channel_major[group][:, h, :], in_=sums[c, n // 2][:, n % 2, :],
                func=ACT.Identity, bias=bias[:, col : col + 1],
            )

        def finish(engine, terms, heads, out, tile_no):
            cos_term = terms[0][:, heads, :].rearrange("p h (j e) -> p (h j) e", e=2)
            sin_term = terms[1][:, heads, :].rearrange("p h (j e) -> p (h j) e", e=2)
            engine.tensor_tensor(out=cos_term, in0=cos_term, in1=sin_term[:, :, ::-1], op=ALU.add)
            nc.sync.dma_start(
                out=out[tile_no * P : (tile_no + 1) * P, heads.start * HEAD_DIM : heads.stop * HEAD_DIM],
                in_=terms[0][:, heads, :].rearrange("p h d -> p (h d)"),
            )

        chunks = 2 * TILES
        for c in range(2):
            for j in range(3):
                project(c, j, token_bank)
                if (c, j) != (1, 2):
                    add_bias(c, 2 * j)
                    add_bias(c, 2 * j + 1)

        for s in range(2 * TILES):
            proj, tile_no = divmod(s, TILES)
            frame, half = divmod(tile_no, 2)
            if s + 1 < chunks:
                add_bias(s + 1, 4)
                add_bias(s + 1, 5)

            token_major = []
            stats = work.tile([P, 8], F32, name="stats", bufs=3)
            for b in range(BANKS):
                bank = token_bank([P, HEADS_PER_BANK, HEAD_DIM])
                token_major.append(bank)
                for i in range(HEADS_PER_BANK):
                    h = HEADS_PER_BANK * b + i
                    nc.tensor.transpose(
                        bank[:, i, :], channel_major[s // 2][:, h, half * P : (half + 1) * P], ident[:]
                    )
                squares = work.tile([P, BANK], BF16, name="squares", bufs=2)
                nc.scalar.activation(
                    out=squares[:], in_=bank[:].rearrange("p h d -> p (h d)"), func=ACT.Square,
                    accum_out=stats[:, b : b + 1],
                )
                if b == BANKS - 1:
                    nc.scalar.activation(
                        out=stats[:, 3:5], in_=stats[:, 0:2], func=ACT.Identity, scale=1.0 / DIM, bias=EPS / 2,
                        accum_out=stats[:, 6:7],
                    )

            more = s + 2 < chunks
            if more:
                for j in range(3):
                    project(s + 2, j, acc_bank)
                add_bias(s + 2, 0)
            rstd = stats[:, 7:8]
            nc.scalar.activation(
                out=rstd, in_=stats[:, 2:3], func=ACT.Abs_reciprocal_sqrt, scale=1.0 / DIM, bias=stats[:, 6:7]
            )
            if more:
                for n in range(1, 4):
                    add_bias(s + 2, n)

            terms = [big_tile([P, HEADS, HEAD_DIM], F32) for kind in range(2)]
            pending = []
            added = 0
            for b in range(BANKS):
                heads = slice(HEADS_PER_BANK * b, HEADS_PER_BANK * (b + 1))
                for kind in range(2):
                    for cols, table in (
                        (slice(0, F_COLS), table_f[proj][:, kind, frame, heads, :]),
                        (slice(F_COLS, HEAD_DIM), table_hw[proj][:, kind, half, heads, :]),
                    ):
                        nc.vector.scalar_tensor_tensor(
                            out=terms[kind][:, heads, cols], in0=token_major[b][:, :, cols], scalar=rstd,
                            in1=table, op0=ALU.mult, op1=ALU.mult,
                        )
                last = s == 2 * TILES - 1
                if last or b in ADD_AFTER:
                    pending.append(slice(added, heads.stop))
                    added = heads.stop
                    if not last or b == 0:
                        finish(nc.gpsimd, terms, pending.pop(), outs[proj], tile_no)
            for done in pending:
                finish(nc.vector, terms, done, outs[proj], tile_no)
